import numpy as np
import ml_dtypes


def mxq(x, axis, fmt="e4m3"):
    dtype, down = {"e4m3": (ml_dtypes.float8_e4m3fn, 7), "e5m2": (ml_dtypes.float8_e5m2, 14)}[fmt]
    v = np.moveaxis(np.asarray(x, np.float32).astype(ml_dtypes.bfloat16).astype(np.float64), axis, -1)
    blocks = v.reshape(v.shape[:-1] + (-1, 32))
    amax = np.abs(blocks).max(-1, keepdims=True)
    byte = np.maximum(np.where(amax > 0, np.frexp(amax)[1] - 1 + 127, 0) - down, 1)
    scale = np.exp2(byte - 127.0)
    codes = (blocks / scale).astype(np.float32).astype(dtype).astype(np.float64)
    return np.moveaxis((codes * scale).reshape(v.shape), -1, axis)


WIDE = False


def mx_kscale(k):
    if not WIDE:
        return np.ones(k)
    levels = np.array([20, -20, 10, -10, 0])
    a = np.random.permutation(np.resize(levels, k // 512 * 4)).reshape(k // 512, 4)
    idx = np.arange(k)
    return np.exp2(a[idx // 512, idx % 128 // 32])


BF16 = ml_dtypes.bfloat16


def bf(x):
    return np.asarray(x, np.float32).astype(BF16)


def f64(x):
    return np.asarray(x).astype(np.float64)


E, T, K, O = 4, 512, 512, 2048


def setup_inputs():
    s = np.tile(mx_kscale(T), E)[:, None]
    inputs = np.random.standard_normal((E * T, K)) * s
    expert_size = np.full((E,), T)
    weight = np.random.standard_normal((O * E, K))
    weight_scale = np.random.uniform(0.01, 0.05, (O * E, 1))
    g = np.random.standard_normal((E * T, O)) * np.exp2(np.random.randint(-12, 1, (E * T, 1))) * 8.0 / s
    return {"inputs": bf(inputs), "weight": bf(weight), "weight_scale": bf(weight_scale),
            "expert_size": bf(expert_size), "grad_out": bf(g)}


def reference(inputs, weight, weight_scale, expert_size, grad_out):
    n_exp = expert_size.shape[0]
    out_size = weight.shape[0] // n_exp
    in_size = weight.shape[1]
    x3 = f64(inputs).reshape(n_exp, -1, in_size)
    g3 = f64(grad_out).reshape(n_exp, -1, out_size)
    dw3 = mxq(g3, 1, "e5m2").transpose(0, 2, 1) @ mxq(x3, 1, "e4m3")
    return dw3.reshape(-1, in_size) * f64(weight_scale)

@@ -1,0 +1,121 @@
+from contextlib import ExitStack
+
+import concourse.masks as masks
+import concourse.mybir as mybir
+
+F32 = mybir.dt.float32
+BF16 = mybir.dt.bfloat16
+U32 = mybir.dt.uint32
+U8 = mybir.dt.uint8
+E4M3X4 = mybir.dt.float8_e4m3fn_x4
+E5M2X4 = mybir.dt.float8_e5m2_x4
+COPY = mybir.ActivationFunctionType.Copy
+
+E, T, K, O = 4, 512, 512, 2048
+P = 128
+PACK = 4
+ROWS = 4
+UNIT = P * ROWS
+UNITS = O // UNIT
+
+FLOPS = 2 * E * T * K * O
+BYTES = 2 * (E * T * K + E * T * O + E * O) + 4 * E * O * K
+
+
+def tile_granitemoehybridparallelexpertsfp8_kernel(
+    tc, inputs, weight, weight_scale, expert_size, grad_out, out
+):
+    nc = tc.nc
+    x_view = inputs.rearrange("(e p j) k -> e p (j k)", e=E, p=P, j=PACK)
+    g_view = grad_out.rearrange("(e p j) o -> e p (j o)", e=E, p=P, j=PACK)
+    out_view = out.rearrange("(u q m) k -> u q (m k)", q=P, m=ROWS)
+    ws_view = weight_scale.rearrange("(u r) one -> u (r one)", r=UNIT)
+
+    with ExitStack() as ctx:
+        const = ctx.enter_context(tc.tile_pool(name="const", bufs=1))
+        raw = ctx.enter_context(tc.tile_pool(name="raw", bufs=E))
+        grp = ctx.enter_context(tc.tile_pool(name="grp", bufs=4))
+        xq = ctx.enter_context(tc.tile_pool(name="xq", bufs=2))
+        gq = ctx.enter_context(tc.tile_pool(name="gq", bufs=3))
+        stage_pool = ctx.enter_context(tc.tile_pool(name="stage", bufs=10))
+        psum = ctx.enter_context(tc.psum_pool(name="psum", bufs=8))
+
+        ws_rows = const.tile([E * UNITS, UNIT], BF16)
+        nc.scalar.dma_start(out=ws_rows[:], in_=ws_view)
+
+        x_raws = []
+        g_raws = []
+        for e in range(E):
+            x_raw = raw.tile([P, PACK * K], BF16)
+            nc.sync.dma_start(out=x_raw[:], in_=x_view[e])
+            x_raws.append(x_raw)
+            g_raw = raw.tile([P, PACK * O], BF16)
+            nc.sync.dma_start(out=g_raw[:], in_=g_view[e])
+            g_raws.append(g_raw)
+
+        ident = const.tile([P, P], F32)
+        masks.make_identity(nc, ident[:])
+        ws_f32 = const.tile([P, ROWS, P], F32)
+        nc.vector.memset(ws_f32[:], 0.0)
+        nc.vector.tensor_copy(
+            out=ws_f32[0 : E * UNITS],
+            in_=ws_rows[:].rearrange("u (q m) -> u m q", m=ROWS),
+        )
+        ws_ps = psum.tile([P, ROWS, P], F32, tag="bank")
+        for m in range(ROWS):
+            nc.tensor.transpose(ws_ps[:, m, :], ws_f32[:, m, :], ident[:])
+        ws_sb = const.tile([P, E * UNITS, ROWS], F32)
+        nc.vector.tensor_copy(
+            out=ws_sb[:].rearrange("p u m -> p m u"), in_=ws_ps[:, :, 0 : E * UNITS]
+        )
+
+        for e in range(E):
+            x_grouped = grp.tile([P, K, PACK], BF16, tag="grouped", align_bytes=64)
+            nc.vector.tensor_copy(
+                out=x_grouped[:].rearrange("p (c i) t -> p c t i", i=4),
+                in_=x_raws[e][:].rearrange("p (t c i) -> p c t i", t=PACK, i=4),
+            )
+            x_codes = xq.tile([P, K], U32, align_bytes=64)
+            x_scales = xq.tile([P, K], U8, align_bytes=64)
+            nc.vector.quantize_mx(
+                out=x_codes[:].bitcast(E4M3X4),
+                scales=x_scales[:],
+                in_=x_grouped[:].rearrange("p k t -> p (k t)"),
+            )
+            g_units = g_raws[e][:].rearrange(
+                "p (j u q m) -> p u q j m", j=PACK, u=UNITS, q=P, m=ROWS
+            )
+            for u in range(UNITS):
+                g_grouped = grp.tile([P, ROWS, P, PACK], BF16, tag="grouped", align_bytes=64)
+                nc.vector.tensor_copy(
+                    out=g_grouped[:].rearrange("p m q j -> p q j m"), in_=g_units[:, u]
+                )
+                g_codes = gq.tile([P, UNIT], U32, align_bytes=64)
+                g_scales = gq.tile([P, UNIT], U8, align_bytes=64)
+                nc.vector.quantize_mx(
+                    out=g_codes[:].bitcast(E5M2X4),
+                    scales=g_scales[:],
+                    in_=g_grouped[:].rearrange("p m q j -> p (m q j)"),
+                )
+                stage = stage_pool.tile([P, ROWS, K], F32)
+                for m in range(ROWS):
+                    cols = slice(m * P, (m + 1) * P)
+                    acc = psum.tile([P, K], F32, tag="bank")
+                    nc.tensor.matmul_mx(
+                        out=acc[:],
+                        lhsT=g_codes[:, cols].bitcast(E5M2X4),
+                        lhsT_scale=g_scales[:, cols],
+                        rhs=x_codes[:].bitcast(E4M3X4),
+                        rhs_scale=x_scales[:],
+                        start=True,
+                        stop=True,
+                    )
+                    nc.scalar.activation(
+                        out=stage[:, m, :],
+                        in_=acc[:],
+                        func=COPY,
+                        scale=ws_sb[:, e * UNITS + u, m : m + 1],
+                    )
+                nc.sync.dma_start(
+                    out=out_view[e * UNITS + u], in_=stage[:].rearrange("p m k -> p (m k)")
+                )

@@ -27,13 +27,14 @@ def tile_granitemoehybridparallelexpertsfp8_kernel(
 ):
     nc = tc.nc
     x_view = inputs.rearrange("(e p j) k -> e p (j k)", e=E, p=P, j=PACK)
-    g_view = grad_out.rearrange("(e p j) o -> e p (j o)", e=E, p=P, j=PACK)
+    g_view = grad_out.rearrange("(e p j) o -> e p j o", e=E, p=P, j=PACK)
     out_view = out.rearrange("(u q m) k -> u q (m k)", q=P, m=ROWS)
     ws_view = weight_scale.rearrange("(u r) one -> u (r one)", r=UNIT)
 
     with ExitStack() as ctx:
         const = ctx.enter_context(tc.tile_pool(name="const", bufs=1))
         raw = ctx.enter_context(tc.tile_pool(name="raw", bufs=E))
+        head = ctx.enter_context(tc.tile_pool(name="head", bufs=1))
         grp = ctx.enter_context(tc.tile_pool(name="grp", bufs=4))
         xq = ctx.enter_context(tc.tile_pool(name="xq", bufs=2))
         gq = ctx.enter_context(tc.tile_pool(name="gq", bufs=3))
@@ -49,9 +50,16 @@ def tile_granitemoehybridparallelexpertsfp8_kernel(
             x_raw = raw.tile([P, PACK * K], BF16)
             nc.sync.dma_start(out=x_raw[:], in_=x_view[e])
             x_raws.append(x_raw)
-            g_raw = raw.tile([P, PACK * O], BF16)
-            nc.sync.dma_start(out=g_raw[:], in_=g_view[e])
-            g_raws.append(g_raw)
+            if e == 0:
+                g_first = head.tile([P, PACK, UNIT], BF16)
+                nc.sync.dma_start(out=g_first[:], in_=g_view[e][:, :, 0:UNIT])
+                g_rest = head.tile([P, PACK, O - UNIT], BF16)
+                nc.sync.dma_start(out=g_rest[:], in_=g_view[e][:, :, UNIT:O])
+                g_raws.append([g_first[:]] + [g_rest[:, :, (u - 1) * UNIT : u * UNIT] for u in range(1, UNITS)])
+            else:
+                g_raw = raw.tile([P, PACK, O], BF16, bufs=E - 1)
+                nc.sync.dma_start(out=g_raw[:], in_=g_view[e])
+                g_raws.append([g_raw[:, :, u * UNIT : (u + 1) * UNIT] for u in range(UNITS)])
 
         ident = const.tile([P, P], F32)
         masks.make_identity(nc, ident[:])
@@ -82,13 +90,11 @@ def tile_granitemoehybridparallelexpertsfp8_kernel(
                 scales=x_scales[:],
                 in_=x_grouped[:].rearrange("p k t -> p (k t)"),
             )
-            g_units = g_raws[e][:].rearrange(
-                "p (j u q m) -> p u q j m", j=PACK, u=UNITS, q=P, m=ROWS
-            )
             for u in range(UNITS):
                 g_grouped = grp.tile([P, ROWS, P, PACK], BF16, tag="grouped", align_bytes=64)
                 nc.vector.tensor_copy(
-                    out=g_grouped[:].rearrange("p m q j -> p q j m"), in_=g_units[:, u]
+                    out=g_grouped[:].rearrange("p m q j -> p q j m"),
+                    in_=g_raws[e][u].rearrange("p j (q m) -> p q j m", m=ROWS),
                 )
                 g_codes = gq.tile([P, UNIT], U32, align_bytes=64)
                 g_scales = gq.tile([P, UNIT], U8, align_bytes=64)

@@ -1,6 +1,5 @@
 from contextlib import ExitStack
 
-import concourse.masks as masks
 import concourse.mybir as mybir
 
 F32 = mybir.dt.float32
@@ -14,9 +13,9 @@ COPY = mybir.ActivationFunctionType.Copy
 E, T, K, O = 4, 512, 512, 2048
 P = 128
 PACK = 4
-ROWS = 4
-UNIT = P * ROWS
-UNITS = O // UNIT
+ROWS = O // P
+SUB = 4
+STORES = [[(0, 16)], [(0, 16)], [(0, 16)], [(0, 8), (8, 12), (12, 16)]]
 
 FLOPS = 2 * E * T * K * O
 BYTES = 2 * (E * T * K + E * T * O + E * O) + 4 * E * O * K
@@ -27,22 +26,21 @@ def tile_granitemoehybridparallelexpertsfp8_kernel(
 ):
     nc = tc.nc
     x_view = inputs.rearrange("(e p j) k -> e p (j k)", e=E, p=P, j=PACK)
-    g_view = grad_out.rearrange("(e p j) o -> e p j o", e=E, p=P, j=PACK)
-    out_view = out.rearrange("(u q m) k -> u q (m k)", q=P, m=ROWS)
-    ws_view = weight_scale.rearrange("(u r) one -> u (r one)", r=UNIT)
+    g_view = grad_out.rearrange("(e p j) o -> e p (j o)", e=E, p=P, j=PACK)
+    out_view = out.rearrange("(e q c) k -> e q c k", e=E, q=P, c=ROWS)
+    ws_view = weight_scale.rearrange("(e q c) one -> q e (c one)", e=E, q=P, c=ROWS)
 
     with ExitStack() as ctx:
         const = ctx.enter_context(tc.tile_pool(name="const", bufs=1))
         raw = ctx.enter_context(tc.tile_pool(name="raw", bufs=E))
-        head = ctx.enter_context(tc.tile_pool(name="head", bufs=1))
         grp = ctx.enter_context(tc.tile_pool(name="grp", bufs=4))
         xq = ctx.enter_context(tc.tile_pool(name="xq", bufs=2))
         gq = ctx.enter_context(tc.tile_pool(name="gq", bufs=3))
-        stage_pool = ctx.enter_context(tc.tile_pool(name="stage", bufs=10))
+        stage_pool = ctx.enter_context(tc.tile_pool(name="stage", bufs=3))
         psum = ctx.enter_context(tc.psum_pool(name="psum", bufs=8))
 
-        ws_rows = const.tile([E * UNITS, UNIT], BF16)
-        nc.scalar.dma_start(out=ws_rows[:], in_=ws_view)
+        ws_bf = const.tile([P, E, ROWS], BF16)
+        nc.scalar.dma_start(out=ws_bf[:], in_=ws_view)
 
         x_raws = []
         g_raws = []
@@ -50,32 +48,12 @@ def tile_granitemoehybridparallelexpertsfp8_kernel(
             x_raw = raw.tile([P, PACK * K], BF16)
             nc.sync.dma_start(out=x_raw[:], in_=x_view[e])
             x_raws.append(x_raw)
-            if e == 0:
-                g_first = head.tile([P, PACK, UNIT], BF16)
-                nc.sync.dma_start(out=g_first[:], in_=g_view[e][:, :, 0:UNIT])
-                g_rest = head.tile([P, PACK, O - UNIT], BF16)
-                nc.sync.dma_start(out=g_rest[:], in_=g_view[e][:, :, UNIT:O])
-                g_raws.append([g_first[:]] + [g_rest[:, :, (u - 1) * UNIT : u * UNIT] for u in range(1, UNITS)])
-            else:
-                g_raw = raw.tile([P, PACK, O], BF16, bufs=E - 1)
-                nc.sync.dma_start(out=g_raw[:], in_=g_view[e])
-                g_raws.append([g_raw[:, :, u * UNIT : (u + 1) * UNIT] for u in range(UNITS)])
+            g_raw = raw.tile([P, PACK * O], BF16)
+            nc.sync.dma_start(out=g_raw[:], in_=g_view[e])
+            g_raws.append(g_raw)
 
-        ident = const.tile([P, P], F32)
-        masks.make_identity(nc, ident[:])
-        ws_f32 = const.tile([P, ROWS, P], F32)
-        nc.vector.memset(ws_f32[:], 0.0)
-        nc.vector.tensor_copy(
-            out=ws_f32[0 : E * UNITS],
-            in_=ws_rows[:].rearrange("u (q m) -> u m q", m=ROWS),
-        )
-        ws_ps = psum.tile([P, ROWS, P], F32, tag="bank")
-        for m in range(ROWS):
-            nc.tensor.transpose(ws_ps[:, m, :], ws_f32[:, m, :], ident[:])
-        ws_sb = const.tile([P, E * UNITS, ROWS], F32)
-        nc.vector.tensor_copy(
-            out=ws_sb[:].rearrange("p u m -> p m u"), in_=ws_ps[:, :, 0 : E * UNITS]
-        )
+        ws_sb = const.tile([P, E, ROWS], F32)
+        nc.vector.tensor_copy(out=ws_sb[:], in_=ws_bf[:])
 
         for e in range(E):
             x_grouped = grp.tile([P, K, PACK], BF16, tag="grouped", align_bytes=64)
@@ -90,23 +68,26 @@ def tile_granitemoehybridparallelexpertsfp8_kernel(
                 scales=x_scales[:],
                 in_=x_grouped[:].rearrange("p k t -> p (k t)"),
             )
-            for u in range(UNITS):
-                g_grouped = grp.tile([P, ROWS, P, PACK], BF16, tag="grouped", align_bytes=64)
+            g_subs = g_raws[e][:].rearrange(
+                "p (j q a m) -> p a q j m", j=PACK, q=P, a=ROWS // SUB, m=SUB
+            )
+            stage = stage_pool.tile([P, ROWS, K], F32)
+            for a in range(ROWS // SUB):
+                g_grouped = grp.tile([P, SUB, P, PACK], BF16, tag="grouped", align_bytes=64)
                 nc.vector.tensor_copy(
-                    out=g_grouped[:].rearrange("p m q j -> p q j m"),
-                    in_=g_raws[e][u].rearrange("p j (q m) -> p q j m", m=ROWS),
+                    out=g_grouped[:].rearrange("p m q j -> p q j m"), in_=g_subs[:, a]
                 )
-                g_codes = gq.tile([P, UNIT], U32, align_bytes=64)
-                g_scales = gq.tile([P, UNIT], U8, align_bytes=64)
+                g_codes = gq.tile([P, SUB * P], U32, align_bytes=64)
+                g_scales = gq.tile([P, SUB * P], U8, align_bytes=64)
                 nc.vector.quantize_mx(
                     out=g_codes[:].bitcast(E5M2X4),
                     scales=g_scales[:],
                     in_=g_grouped[:].rearrange("p m q j -> p (m q j)"),
                 )
-                stage = stage_pool.tile([P, ROWS, K], F32)
-                for m in range(ROWS):
+                for m in range(SUB):
+                    c = a * SUB + m
                     cols = slice(m * P, (m + 1) * P)
-                    acc = psum.tile([P, K], F32, tag="bank")
+                    acc = psum.tile([P, K], F32)
                     nc.tensor.matmul_mx(
                         out=acc[:],
                         lhsT=g_codes[:, cols].bitcast(E5M2X4),
@@ -117,11 +98,8 @@ def tile_granitemoehybridparallelexpertsfp8_kernel(
                         stop=True,
                     )
                     nc.scalar.activation(
-                        out=stage[:, m, :],
-                        in_=acc[:],
-                        func=COPY,
-                        scale=ws_sb[:, e * UNITS + u, m : m + 1],
+                        out=stage[:, c, :], in_=acc[:], func=COPY, scale=ws_sb[:, e, c : c + 1]
                     )
-                nc.sync.dma_start(
-                    out=out_view[e * UNITS + u], in_=stage[:].rearrange("p m k -> p (m k)")
-                )
+                    for c0, c1 in STORES[e]:
+                        if c1 == c + 1:
+                            nc.sync.dma_start(out=out_view[e][:, c0:c1, :], in_=stage[:, c0:c1, :])

@@ -1,5 +1,6 @@
 from contextlib import ExitStack
 
+import concourse.masks as masks
 import concourse.mybir as mybir
 
 F32 = mybir.dt.float32
@@ -28,7 +29,7 @@ def tile_granitemoehybridparallelexpertsfp8_kernel(
     x_view = inputs.rearrange("(e p j) k -> e p (j k)", e=E, p=P, j=PACK)
     g_view = grad_out.rearrange("(e p j) o -> e p (j o)", e=E, p=P, j=PACK)
     out_view = out.rearrange("(e q c) k -> e q c k", e=E, q=P, c=ROWS)
-    ws_view = weight_scale.rearrange("(e q c) one -> q e (c one)", e=E, q=P, c=ROWS)
+    ws_view = weight_scale.rearrange("(e r) one -> e (r one)", e=E)
 
     with ExitStack() as ctx:
         const = ctx.enter_context(tc.tile_pool(name="const", bufs=1))
@@ -39,8 +40,9 @@ def tile_granitemoehybridparallelexpertsfp8_kernel(
         stage_pool = ctx.enter_context(tc.tile_pool(name="stage", bufs=3))
         psum = ctx.enter_context(tc.psum_pool(name="psum", bufs=8))
 
-        ws_bf = const.tile([P, E, ROWS], BF16)
-        nc.scalar.dma_start(out=ws_bf[:], in_=ws_view)
+        ws_rows = const.tile([P, O], BF16)
+        nc.vector.memset(ws_rows[:], 0.0)
+        nc.scalar.dma_start(out=ws_rows[0:E, :], in_=ws_view)
 
         x_raws = []
         g_raws = []
@@ -52,8 +54,18 @@ def tile_granitemoehybridparallelexpertsfp8_kernel(
             nc.sync.dma_start(out=g_raw[:], in_=g_view[e])
             g_raws.append(g_raw)
 
+        ident = const.tile([P, P], BF16)
+        masks.make_identity(nc, ident[:])
+        ws_cols = ws_rows[:].rearrange("p (q c) -> p c q", c=ROWS)
         ws_sb = const.tile([P, E, ROWS], F32)
-        nc.vector.tensor_copy(out=ws_sb[:], in_=ws_bf[:])
+        for h in range(2):
+            ws_ps = psum.tile([P, ROWS // 2, P], BF16, tag="acc")
+            for i in range(ROWS // 2):
+                nc.tensor.transpose(ws_ps[:, i, :], ws_cols[:, h * (ROWS // 2) + i, :], ident[:])
+            nc.vector.tensor_copy(
+                out=ws_sb[:, :, h * (ROWS // 2) : (h + 1) * (ROWS // 2)].rearrange("p e c -> p c e"),
+                in_=ws_ps[:, :, 0:E],
+            )
 
         for e in range(E):
             x_grouped = grp.tile([P, K, PACK], BF16, tag="grouped", align_bytes=64)
@@ -87,7 +99,7 @@ def tile_granitemoehybridparallelexpertsfp8_kernel(
                 for m in range(SUB):
                     c = a * SUB + m
                     cols = slice(m * P, (m + 1) * P)
-                    acc = psum.tile([P, K], F32)
+                    acc = psum.tile([P, K], F32, tag="acc")
                     nc.tensor.matmul_mx(
                         out=acc[:],
                         lhsT=g_codes[:, cols].bitcast(E5M2X4),

from contextlib import ExitStack

import concourse.masks as masks
import concourse.mybir as mybir

F32 = mybir.dt.float32
BF16 = mybir.dt.bfloat16
U32 = mybir.dt.uint32
U8 = mybir.dt.uint8
E4M3X4 = mybir.dt.float8_e4m3fn_x4
E5M2X4 = mybir.dt.float8_e5m2_x4
COPY = mybir.ActivationFunctionType.Copy

E, T, K, O = 4, 512, 512, 2048
P = 128
PACK = 4
ROWS = O // P
SUB = 4
STORES = [[(0, 16)], [(0, 16)], [(0, 16)], [(0, 8), (8, 12), (12, 16)]]

FLOPS = 2 * E * T * K * O
BYTES = 2 * (E * T * K + E * T * O + E * O) + 4 * E * O * K


def tile_granitemoehybridparallelexpertsfp8_kernel(
    tc, inputs, weight, weight_scale, expert_size, grad_out, out
):
    nc = tc.nc
    x_view = inputs.rearrange("(e p j) k -> e p (j k)", e=E, p=P, j=PACK)
    g_view = grad_out.rearrange("(e p j) o -> e p (j o)", e=E, p=P, j=PACK)
    out_view = out.rearrange("(e q c) k -> e q c k", e=E, q=P, c=ROWS)
    ws_view = weight_scale.rearrange("(e r) one -> e (r one)", e=E)

    with ExitStack() as ctx:
        const = ctx.enter_context(tc.tile_pool(name="const", bufs=1))
        raw = ctx.enter_context(tc.tile_pool(name="raw", bufs=E))
        grp = ctx.enter_context(tc.tile_pool(name="grp", bufs=4))
        xq = ctx.enter_context(tc.tile_pool(name="xq", bufs=2))
        gq = ctx.enter_context(tc.tile_pool(name="gq", bufs=3))
        stage_pool = ctx.enter_context(tc.tile_pool(name="stage", bufs=3))
        psum = ctx.enter_context(tc.psum_pool(name="psum", bufs=8))

        ws_rows = const.tile([P, O], BF16)
        nc.vector.memset(ws_rows[:], 0.0)
        nc.scalar.dma_start(out=ws_rows[0:E, :], in_=ws_view)

        x_raws = []
        g_raws = []
        for e in range(E):
            x_raw = raw.tile([P, PACK * K], BF16)
            nc.sync.dma_start(out=x_raw[:], in_=x_view[e])
            x_raws.append(x_raw)
            g_raw = raw.tile([P, PACK * O], BF16)
            nc.sync.dma_start(out=g_raw[:], in_=g_view[e])
            g_raws.append(g_raw)

        ident = const.tile([P, P], BF16)
        masks.make_identity(nc, ident[:])
        ws_cols = ws_rows[:].rearrange("p (q c) -> p c q", c=ROWS)
        ws_sb = const.tile([P, E, ROWS], F32)
        for h in range(2):
            ws_ps = psum.tile([P, ROWS // 2, P], BF16, tag="acc")
            for i in range(ROWS // 2):
                nc.tensor.transpose(ws_ps[:, i, :], ws_cols[:, h * (ROWS // 2) + i, :], ident[:])
            nc.vector.tensor_copy(
                out=ws_sb[:, :, h * (ROWS // 2) : (h + 1) * (ROWS // 2)].rearrange("p e c -> p c e"),
                in_=ws_ps[:, :, 0:E],
            )

        for e in range(E):
            x_grouped = grp.tile([P, K, PACK], BF16, tag="grouped", align_bytes=64)
            nc.vector.tensor_copy(
                out=x_grouped[:].rearrange("p (c i) t -> p c t i", i=4),
                in_=x_raws[e][:].rearrange("p (t c i) -> p c t i", t=PACK, i=4),
            )
            x_codes = xq.tile([P, K], U32, align_bytes=64)
            x_scales = xq.tile([P, K], U8, align_bytes=64)
            nc.vector.quantize_mx(
                out=x_codes[:].bitcast(E4M3X4),
                scales=x_scales[:],
                in_=x_grouped[:].rearrange("p k t -> p (k t)"),
            )
            g_subs = g_raws[e][:].rearrange(
                "p (j q a m) -> p a q j m", j=PACK, q=P, a=ROWS // SUB, m=SUB
            )
            stage = stage_pool.tile([P, ROWS, K], F32)
            for a in range(ROWS // SUB):
                g_grouped = grp.tile([P, SUB, P, PACK], BF16, tag="grouped", align_bytes=64)
                nc.vector.tensor_copy(
                    out=g_grouped[:].rearrange("p m q j -> p q j m"), in_=g_subs[:, a]
                )
                g_codes = gq.tile([P, SUB * P], U32, align_bytes=64)
                g_scales = gq.tile([P, SUB * P], U8, align_bytes=64)
                nc.vector.quantize_mx(
                    out=g_codes[:].bitcast(E5M2X4),
                    scales=g_scales[:],
                    in_=g_grouped[:].rearrange("p m q j -> p (m q j)"),
                )
                for m in range(SUB):
                    c = a * SUB + m
                    cols = slice(m * P, (m + 1) * P)
                    acc = psum.tile([P, K], F32, tag="acc")
                    nc.tensor.matmul_mx(
                        out=acc[:],
                        lhsT=g_codes[:, cols].bitcast(E5M2X4),
                        lhsT_scale=g_scales[:, cols],
                        rhs=x_codes[:].bitcast(E4M3X4),
                        rhs_scale=x_scales[:],
                        start=True,
                        stop=True,
                    )
                    nc.scalar.activation(
                        out=stage[:, c, :], in_=acc[:], func=COPY, scale=ws_sb[:, e, c : c + 1]
                    )
                    for c0, c1 in STORES[e]:
                        if c1 == c + 1:
                            nc.sync.dma_start(out=out_view[e][:, c0:c1, :], in_=stage[:, c0:c1, :])
